import numpy as np
import ml_dtypes


def mxq(x, axis, fmt="e4m3"):
    dtype, down = {"e4m3": (ml_dtypes.float8_e4m3fn, 7), "e5m2": (ml_dtypes.float8_e5m2, 14)}[fmt]
    v = np.moveaxis(np.asarray(x, np.float32).astype(ml_dtypes.bfloat16).astype(np.float64), axis, -1)
    blocks = v.reshape(v.shape[:-1] + (-1, 32))
    amax = np.abs(blocks).max(-1, keepdims=True)
    byte = np.maximum(np.where(amax > 0, np.frexp(amax)[1] - 1 + 127, 0) - down, 1)
    scale = np.exp2(byte - 127.0)
    codes = (blocks / scale).astype(np.float32).astype(dtype).astype(np.float64)
    return np.moveaxis((codes * scale).reshape(v.shape), -1, axis)


WIDE = False


def mx_kscale(k):
    if not WIDE:
        return np.ones(k)
    levels = np.array([10, -10, 5, -5, 0])
    a = np.random.permutation(np.resize(levels, k // 512 * 4)).reshape(k // 512, 4)
    idx = np.arange(k)
    return np.exp2(a[idx // 512, idx % 128 // 32])


BF16 = ml_dtypes.bfloat16


def bf(x):
    return np.asarray(x, np.float32).astype(BF16)


def f64(x):
    return np.asarray(x).astype(np.float64)


E2M1 = np.array([0.0, 0.5, 1.0, 1.5, 2.0, 3.0, 4.0, 6.0, -0.0, -0.5, -1.0, -1.5, -2.0, -3.0, -4.0, -6.0])


def pack_weight(w, fmt):
    k, n = w.shape
    w = f64(bf(w)).reshape(k // 32, 32, n)
    amax = np.abs(w).max(1)
    if fmt == "e4m3":
        byte = np.frexp(amax)[1] - 1 + 127 - 7
    else:
        mant, ex = np.frexp(amax / 6.0)
        byte = np.where(mant > 0.5, ex, ex - 1) + 127
    byte = np.clip(np.where(amax > 0, byte, 1), 1, 254)
    scaled = (w * np.exp2(127.0 - byte)[:, None, :]).reshape(k, n).astype(np.float32)
    by_word = np.ascontiguousarray(scaled.reshape(k // 512, 128, 4, n).transpose(0, 1, 3, 2))
    if fmt == "e4m3":
        words = by_word.astype(ml_dtypes.float8_e4m3fn).view(np.uint8)
    else:
        c = by_word.astype(ml_dtypes.float4_e2m1fn).view(np.uint8) & 0xF
        words = c[..., 0::2] | (c[..., 1::2] << 4)
    return np.ascontiguousarray(words), np.ascontiguousarray(byte.astype(np.uint8).reshape(k // 512, 16, n))


def unpack_weight(words, scales, fmt):
    g, p, n, _ = words.shape
    if fmt == "e4m3":
        vals = np.ascontiguousarray(words).view(ml_dtypes.float8_e4m3fn).astype(np.float64)
    else:
        nib = np.empty((g, p, n, 4), np.uint8)
        nib[..., 0::2] = words & 0xF
        nib[..., 1::2] = words >> 4
        vals = E2M1[nib]
    vals = vals * np.repeat(np.exp2(scales.astype(np.float64) - 127.0), 8, axis=1)[..., None]
    return vals.transpose(0, 1, 3, 2).reshape(g * 512, n)

def pack4(w):
    words, scales = pack_weight(w, "e2m1")
    return words.reshape(words.shape[0], 128, -1), scales


def unpack4(words, scales):
    return unpack_weight(words.reshape(words.shape[0], 128, -1, 2), scales, "e2m1")


B, D0, D1, D2, D3 = 512, 2048, 2048, 2048, 2048
HEBB = 0.01
RATE = 0.001
BATCH_NUM = 1
C = HEBB * RATE / BATCH_NUM


def centred(s):
    return s / np.exp2(np.round(np.log2(s.mean())))


def setup_inputs():
    s = centred(mx_kscale(D2))
    vi = bf(np.maximum(3.0 + 5.0 * np.random.standard_normal((B, D2)), 0.0) * s)
    w = np.random.standard_normal((D3, D2)) * 0.9 / np.sqrt(D2) / s[None, :]
    words, scales = pack4(w.T)
    b = bf(3.0 + 1.5 * np.random.standard_normal(D3))
    return {"vi": vi, "W_words": words, "W_scales": scales, "b": b}


def reference(vi, W_words, W_scales, b):
    vi = f64(vi)
    vj = np.maximum((mxq(vi, 1, "e4m3") @ unpack4(W_words, W_scales)) + f64(b), 0.0)
    m = np.mean(vj, axis=0)
    out = vj + np.sum(vi, axis=1, keepdims=True) * (C * m)[None, :]
    return out, m

@@ -1,0 +1,223 @@
+from contextlib import ExitStack
+
+import concourse.mybir as mybir
+from concourse.masks import make_identity
+
+F32 = mybir.dt.float32
+BF16 = mybir.dt.bfloat16
+I32 = mybir.dt.int32
+U32 = mybir.dt.uint32
+U8 = mybir.dt.uint8
+FP8X4 = mybir.dt.float8_e4m3fn_x4
+FP4X4 = mybir.dt.float4_e2m1fn_x4
+FUNC = mybir.ActivationFunctionType
+ALU = mybir.AluOpType
+AXIS = mybir.AxisListType
+
+P = 128
+PACK = 4
+K_PASS = P * PACK
+ROWS = 512
+K = 2048
+OUTS = 2048
+ROW_TILES = ROWS // P
+PASSES = K // K_PASS
+OUT_TILES = OUTS // P
+C = 0.01 * 0.001 / 1
+
+RUN = 4
+ROUNDS = OUT_TILES // RUN
+LAG = 2
+STORE_TILES = 2
+
+FLOPS = 2 * ROWS * K * OUTS
+
+
+def tile_optimalnet_pb_kernel(tc, vi, W_words, W_scales, b, out_0, out_1):
+    nc = tc.nc
+    with ExitStack() as stack:
+        stack.enter_context(tc.manual_schedule())
+        keep = stack.enter_context(tc.tile_pool(name="keep", bufs=1))
+        layer = stack.enter_context(tc.tile_pool(name="layer", bufs=2 * RUN))
+        leaving = stack.enter_context(tc.tile_pool(name="leaving", bufs=4))
+        sums_psum = stack.enter_context(tc.psum_pool(name="sums_psum", bufs=4))
+        turn_psum = stack.enter_context(tc.psum_pool(name="turn_psum", bufs=4))
+
+        ident = keep.tile([P, P], F32)
+        make_identity(nc, ident[:])
+        b_rows = keep.tile([P, P], BF16)
+        nc.vector.memset(b_rows[:], 0.0)
+        col_sums = keep.tile([P, P], F32)
+        nc.vector.memset(col_sums[:], 0.0)
+        w_planes = []
+        for rnd in range(ROUNDS):
+            planes = keep.tile([P, PASSES, RUN * P], U8, name="w_planes%d" % rnd, align_bytes=64)
+            nc.vector.memset(planes[:].bitcast(I32), 0)
+            w_planes.append(planes)
+
+        nc.scalar.dma_start(out=b_rows[0:OUT_TILES, :], in_=b.rearrange("(j p) -> j p", p=P))
+        x_tiles = []
+        for rt in range(ROW_TILES):
+            x = keep.tile([P, K], BF16, name="x%d" % rt)
+            nc.sync.dma_start(out=x[:], in_=vi[rt * P : (rt + 1) * P, :])
+            x_tiles.append(x)
+        words_dram = W_words.bitcast(I32).rearrange("g p n -> p g n")
+        scales_dram = W_scales.bitcast(I32).rearrange("g (q r) n -> r q g n", r=4)
+        w_words = []
+        for rnd in range(ROUNDS):
+            plane_cols = slice(rnd * RUN * P // 4, (rnd + 1) * RUN * P // 4)
+            for r in range(4):
+                nc.sync.dma_start(
+                    out=w_planes[rnd][:].bitcast(I32)[r:P:32], in_=scales_dram[r][:, :, plane_cols]
+                )
+            words = keep.tile([P, PASSES, RUN * P * 2], U8, name="w_words%d" % rnd, align_bytes=64)
+            word_cols = slice(rnd * RUN * P // 2, (rnd + 1) * RUN * P // 2)
+            nc.sync.dma_start(out=words[:].bitcast(I32), in_=words_dram[:, :, word_cols])
+            w_words.append(words)
+
+        b_square = keep.tile([P, P], F32)
+        nc.vector.tensor_copy(out=b_square[:], in_=b_rows[:])
+        b_bank = turn_psum.tile([P, P], F32, tag="turn")
+        nc.tensor.transpose(b_bank[:], b_square[:], ident[:])
+        bias = keep.tile([P, OUT_TILES], F32)
+        nc.vector.tensor_copy(out=bias[:], in_=b_bank[:, 0:OUT_TILES])
+
+        grouped = keep.tile([P, PASSES, ROWS, PACK], BF16, align_bytes=64)
+        grouped_words = grouped[:].bitcast(F32)
+        vi_codes = keep.tile([P, PASSES, ROWS], U32, align_bytes=64)
+        vi_planes = keep.tile([P, PASSES, ROWS], U8, align_bytes=64)
+        words_a_pass = K_PASS // 2
+        for rt in range(ROW_TILES):
+            x_words = x_tiles[rt][:].bitcast(F32)
+            rows = slice(rt * P, (rt + 1) * P)
+            for first in range(0, PASSES, 2):
+                bank = turn_psum.tile([P, 2, 2, P], F32, tag="turn")
+                for gi in range(2):
+                    start_word = (first + gi) * words_a_pass
+                    for u in range(2):
+                        nc.tensor.transpose(
+                            bank[:, gi, u, :],
+                            x_words[:, start_word + u : start_word + words_a_pass : 2],
+                            ident[:],
+                        )
+                nc.scalar.copy(
+                    out=grouped_words[:, first : first + 2, rows, :],
+                    in_=bank[:].rearrange("p g u r -> p g r u"),
+                )
+            for g in range(PASSES):
+                nc.vector.quantize_mx(
+                    out=vi_codes[:, g, rows].bitcast(FP8X4),
+                    scales=vi_planes[:, g, rows],
+                    in_=grouped[:, g, rows, :].rearrange("p r t -> p (r t)"),
+                )
+
+        half = ROW_TILES // 2
+        row_sums_v = keep.tile([P, half], F32)
+        row_sums_s = keep.tile([P, half], F32)
+        unused = keep.tile([P, K], BF16)
+        for i in range(half):
+            nc.vector.tensor_reduce(
+                out=row_sums_v[:, i : i + 1], in_=x_tiles[i][:], axis=AXIS.X, op=ALU.add
+            )
+            nc.scalar.activation(
+                out=unused[:],
+                in_=x_tiles[half + i][:],
+                func=FUNC.Copy,
+                accum_out=row_sums_s[:, i : i + 1],
+            )
+        row_factor = keep.tile([P, ROWS], F32)
+
+        def spread_row_sums():
+            repeated = keep.tile([P, ROW_TILES, P], F32)
+            nc.vector.tensor_copy(
+                out=repeated[:, 0:half, :], in_=row_sums_v[:].unsqueeze(2).to_broadcast([P, half, P])
+            )
+            nc.vector.tensor_copy(
+                out=repeated[:, half:ROW_TILES, :],
+                in_=row_sums_s[:].unsqueeze(2).to_broadcast([P, half, P]),
+            )
+            bank = turn_psum.tile([P, ROW_TILES, P], F32, tag="turn")
+            for rt in range(ROW_TILES):
+                nc.tensor.transpose(bank[:, rt, :], repeated[:, rt, :], ident[:])
+            nc.vector.tensor_scalar(
+                out=row_factor[:],
+                in0=bank[:].rearrange("p t r -> p (t r)"),
+                scalar1=C / ROWS,
+                scalar2=None,
+                op0=ALU.mult,
+            )
+
+        vj_tiles = {}
+
+        def multiply(j):
+            rnd, i = divmod(j, RUN)
+            acc = sums_psum.tile([P, ROWS], F32, tag="acc")
+            for g in range(PASSES):
+                nc.tensor.matmul_mx(
+                    out=acc[:],
+                    lhsT=w_words[rnd][:, g, i * P * 2 : (i + 1) * P * 2].bitcast(FP4X4),
+                    lhsT_scale=w_planes[rnd][:, g, i * P : (i + 1) * P],
+                    rhs=vi_codes[:, g, :].bitcast(FP8X4),
+                    rhs_scale=vi_planes[:, g, :],
+                    start=(g == 0),
+                    stop=(g == PASSES - 1),
+                )
+            vj = layer.tile([P, ROWS], F32, tag="vj")
+            nc.scalar.activation(
+                out=vj[:],
+                in_=acc[:],
+                func=FUNC.Relu,
+                bias=bias[:, j : j + 1],
+                accum_out=col_sums[:, j : j + 1],
+            )
+            vj_tiles[j] = vj
+
+        def correct(j):
+            vj = vj_tiles[j]
+            nc.vector.scalar_tensor_tensor(
+                out=vj[:],
+                in0=row_factor[:],
+                scalar=col_sums[:, j : j + 1],
+                in1=vj[:],
+                op0=ALU.mult,
+                op1=ALU.add,
+            )
+
+        out_view = out_0.rearrange("(t r) o -> r t o", r=P)
+
+        def turn_back(rnd):
+            for first in range(rnd * RUN, (rnd + 1) * RUN, STORE_TILES):
+                result = leaving.tile([P, ROW_TILES, STORE_TILES * P], F32, tag="result")
+                for i in range(STORE_TILES):
+                    vj = vj_tiles[first + i]
+                    bank = turn_psum.tile([P, ROW_TILES, P], F32, tag="turn")
+                    for rt in range(ROW_TILES):
+                        nc.tensor.transpose(bank[:, rt, :], vj[:, rt * P : (rt + 1) * P], ident[:])
+                    if i % 2 == 0:
+                        nc.scalar.copy(out=result[:, :, i * P : (i + 1) * P], in_=bank[:])
+                    else:
+                        nc.vector.tensor_copy(out=result[:, :, i * P : (i + 1) * P], in_=bank[:])
+                nc.sync.dma_start(
+                    out=out_view[:, :, first * P : (first + STORE_TILES) * P], in_=result[:]
+                )
+
+        for rnd in range(ROUNDS + 1):
+            for i in range(RUN):
+                if rnd < ROUNDS:
+                    multiply(rnd * RUN + i)
+                    if rnd > 0:
+                        correct(rnd * RUN + i)
+                if rnd > 0 and i == LAG - 1:
+                    turn_back(rnd - 1)
+            if rnd == 0:
+                spread_row_sums()
+                for j in range(RUN):
+                    correct(j)
+
+        mean_bank = turn_psum.tile([P, P], F32, tag="turn")
+        nc.tensor.transpose(mean_bank[:], col_sums[:], ident[:])
+        means = keep.tile([P, P], F32)
+        nc.scalar.activation(
+            out=means[0:OUT_TILES, :], in_=mean_bank[0:OUT_TILES, :], func=FUNC.Copy, scale=1.0 / ROWS
+        )
+        nc.sync.dma_start(out=out_1.rearrange("(j p) -> j p", p=P), in_=means[0:OUT_TILES, :])

@@ -27,7 +27,7 @@ C = 0.01 * 0.001 / 1
 
 RUN = 4
 ROUNDS = OUT_TILES // RUN
-LAG = 2
+LAG = 3
 STORE_TILES = 2
 
 FLOPS = 2 * ROWS * K * OUTS
@@ -45,6 +45,8 @@ def tile_optimalnet_pb_kernel(tc, vi, W_words, W_scales, b, out_0, out_1):
 
         ident = keep.tile([P, P], F32)
         make_identity(nc, ident[:])
+        ident_bf16 = keep.tile([P, P], BF16)
+        make_identity(nc, ident_bf16[:])
         b_rows = keep.tile([P, P], BF16)
         nc.vector.memset(b_rows[:], 0.0)
         col_sums = keep.tile([P, P], F32)
@@ -75,18 +77,18 @@ def tile_optimalnet_pb_kernel(tc, vi, W_words, W_scales, b, out_0, out_1):
             nc.sync.dma_start(out=words[:].bitcast(I32), in_=words_dram[:, :, word_cols])
             w_words.append(words)
 
-        b_square = keep.tile([P, P], F32)
-        nc.vector.tensor_copy(out=b_square[:], in_=b_rows[:])
-        b_bank = turn_psum.tile([P, P], F32, tag="turn")
-        nc.tensor.transpose(b_bank[:], b_square[:], ident[:])
-        bias = keep.tile([P, OUT_TILES], F32)
-        nc.vector.tensor_copy(out=bias[:], in_=b_bank[:, 0:OUT_TILES])
-
         grouped = keep.tile([P, PASSES, ROWS, PACK], BF16, align_bytes=64)
         grouped_words = grouped[:].bitcast(F32)
         vi_codes = keep.tile([P, PASSES, ROWS], U32, align_bytes=64)
         vi_planes = keep.tile([P, PASSES, ROWS], U8, align_bytes=64)
         words_a_pass = K_PASS // 2
+        row_sums = []
+        for rt in range(ROW_TILES):
+            row_sums.append(keep.tile([P, 1], F32, name="row_sum%d" % rt))
+
+        def sum_rows_on_vector(rt):
+            nc.vector.tensor_reduce(out=row_sums[rt][:], in_=x_tiles[rt][:], axis=AXIS.X, op=ALU.add)
+
         for rt in range(ROW_TILES):
             x_words = x_tiles[rt][:].bitcast(F32)
             rows = slice(rt * P, (rt + 1) * P)
@@ -104,6 +106,8 @@ def tile_optimalnet_pb_kernel(tc, vi, W_words, W_scales, b, out_0, out_1):
                     out=grouped_words[:, first : first + 2, rows, :],
                     in_=bank[:].rearrange("p g u r -> p g r u"),
                 )
+            if rt == 0:
+                sum_rows_on_vector(rt)
             for g in range(PASSES):
                 nc.vector.quantize_mx(
                     out=vi_codes[:, g, rows].bitcast(FP8X4),
@@ -111,34 +115,26 @@ def tile_optimalnet_pb_kernel(tc, vi, W_words, W_scales, b, out_0, out_1):
                     in_=grouped[:, g, rows, :].rearrange("p r t -> p (r t)"),
                 )
 
-        half = ROW_TILES // 2
-        row_sums_v = keep.tile([P, half], F32)
-        row_sums_s = keep.tile([P, half], F32)
+        b_bank = turn_psum.tile([P, P], BF16, tag="turn")
+        nc.tensor.transpose(b_bank[:], b_rows[:], ident_bf16[:])
+        bias = keep.tile([P, OUT_TILES], F32)
+        nc.scalar.copy(out=bias[:], in_=b_bank[:, 0:OUT_TILES])
+
+        for rt in range(1, ROW_TILES - 1):
+            sum_rows_on_vector(rt)
         unused = keep.tile([P, K], BF16)
-        for i in range(half):
-            nc.vector.tensor_reduce(
-                out=row_sums_v[:, i : i + 1], in_=x_tiles[i][:], axis=AXIS.X, op=ALU.add
-            )
-            nc.scalar.activation(
-                out=unused[:],
-                in_=x_tiles[half + i][:],
-                func=FUNC.Copy,
-                accum_out=row_sums_s[:, i : i + 1],
-            )
+        nc.scalar.activation(
+            out=unused[:],
+            in_=x_tiles[ROW_TILES - 1][:],
+            func=FUNC.Copy,
+            accum_out=row_sums[ROW_TILES - 1][:],
+        )
         row_factor = keep.tile([P, ROWS], F32)
 
         def spread_row_sums():
-            repeated = keep.tile([P, ROW_TILES, P], F32)
-            nc.vector.tensor_copy(
-                out=repeated[:, 0:half, :], in_=row_sums_v[:].unsqueeze(2).to_broadcast([P, half, P])
-            )
-            nc.vector.tensor_copy(
-                out=repeated[:, half:ROW_TILES, :],
-                in_=row_sums_s[:].unsqueeze(2).to_broadcast([P, half, P]),
-            )
             bank = turn_psum.tile([P, ROW_TILES, P], F32, tag="turn")
             for rt in range(ROW_TILES):
-                nc.tensor.transpose(bank[:, rt, :], repeated[:, rt, :], ident[:])
+                nc.tensor.transpose(bank[:, rt, :], row_sums[rt][:].to_broadcast([P, P]), ident[:])
             nc.vector.tensor_scalar(
                 out=row_factor[:],
                 in0=bank[:].rearrange("p t r -> p (t r)"),

@@ -27,8 +27,10 @@ C = 0.01 * 0.001 / 1
 
 RUN = 4
 ROUNDS = OUT_TILES // RUN
-LAG = 3
 STORE_TILES = 2
+HALF_TILES = 2
+HALVES = ROW_TILES // HALF_TILES
+HALF_ROWS = HALF_TILES * P
 
 FLOPS = 2 * ROWS * K * OUTS
 
@@ -38,7 +40,7 @@ def tile_optimalnet_pb_kernel(tc, vi, W_words, W_scales, b, out_0, out_1):
     with ExitStack() as stack:
         stack.enter_context(tc.manual_schedule())
         keep = stack.enter_context(tc.tile_pool(name="keep", bufs=1))
-        layer = stack.enter_context(tc.tile_pool(name="layer", bufs=2 * RUN))
+        layer = stack.enter_context(tc.tile_pool(name="layer", bufs=10))
         leaving = stack.enter_context(tc.tile_pool(name="leaving", bufs=4))
         sums_psum = stack.enter_context(tc.psum_pool(name="sums_psum", bufs=4))
         turn_psum = stack.enter_context(tc.psum_pool(name="turn_psum", bufs=4))
@@ -47,94 +49,104 @@ def tile_optimalnet_pb_kernel(tc, vi, W_words, W_scales, b, out_0, out_1):
         make_identity(nc, ident[:])
         ident_bf16 = keep.tile([P, P], BF16)
         make_identity(nc, ident_bf16[:])
+        w_planes = []
+        for rnd in range(ROUNDS):
+            planes = keep.tile([P, PASSES, RUN * P], U8, name="w_planes%d" % rnd, align_bytes=64)
+            w_planes.append(planes)
+        nc.vector.memset(w_planes[0][:].bitcast(I32), 0)
         b_rows = keep.tile([P, P], BF16)
         nc.vector.memset(b_rows[:], 0.0)
         col_sums = keep.tile([P, P], F32)
         nc.vector.memset(col_sums[:], 0.0)
-        w_planes = []
-        for rnd in range(ROUNDS):
-            planes = keep.tile([P, PASSES, RUN * P], U8, name="w_planes%d" % rnd, align_bytes=64)
-            nc.vector.memset(planes[:].bitcast(I32), 0)
-            w_planes.append(planes)
+        for rnd in range(1, ROUNDS):
+            nc.vector.memset(w_planes[rnd][:].bitcast(I32), 0)
 
         nc.scalar.dma_start(out=b_rows[0:OUT_TILES, :], in_=b.rearrange("(j p) -> j p", p=P))
-        x_tiles = []
-        for rt in range(ROW_TILES):
-            x = keep.tile([P, K], BF16, name="x%d" % rt)
-            nc.sync.dma_start(out=x[:], in_=vi[rt * P : (rt + 1) * P, :])
-            x_tiles.append(x)
+        x_view = vi.rearrange("(h i r) k -> h r i k", i=HALF_TILES, r=P)
+        x_tiles = {}
+
+        def load_x(g):
+            for h in range(HALVES):
+                x = keep.tile([P, HALF_TILES, K_PASS], BF16, name="x%d_%d" % (g, h))
+                nc.sync.dma_start(out=x[:], in_=x_view[h][:, :, g * K_PASS : (g + 1) * K_PASS])
+                x_tiles[(g, h)] = x
+
         words_dram = W_words.bitcast(I32).rearrange("g p n -> p g n")
         scales_dram = W_scales.bitcast(I32).rearrange("g (q r) n -> r q g n", r=4)
-        w_words = []
-        for rnd in range(ROUNDS):
+        w_words = {}
+
+        def load_scales(rnd):
             plane_cols = slice(rnd * RUN * P // 4, (rnd + 1) * RUN * P // 4)
             for r in range(4):
                 nc.sync.dma_start(
                     out=w_planes[rnd][:].bitcast(I32)[r:P:32], in_=scales_dram[r][:, :, plane_cols]
                 )
+
+        def load_words(rnd):
             words = keep.tile([P, PASSES, RUN * P * 2], U8, name="w_words%d" % rnd, align_bytes=64)
             word_cols = slice(rnd * RUN * P // 2, (rnd + 1) * RUN * P // 2)
             nc.sync.dma_start(out=words[:].bitcast(I32), in_=words_dram[:, :, word_cols])
-            w_words.append(words)
+            w_words[rnd] = words
+
+        load_x(0)
+        load_scales(0)
+        load_x(1)
+        load_words(0)
+        load_x(2)
+        load_x(3)
+        for rnd in range(1, ROUNDS):
+            load_scales(rnd)
+            load_words(rnd)
 
         grouped = keep.tile([P, PASSES, ROWS, PACK], BF16, align_bytes=64)
         grouped_words = grouped[:].bitcast(F32)
         vi_codes = keep.tile([P, PASSES, ROWS], U32, align_bytes=64)
         vi_planes = keep.tile([P, PASSES, ROWS], U8, align_bytes=64)
         words_a_pass = K_PASS // 2
-        row_sums = []
-        for rt in range(ROW_TILES):
-            row_sums.append(keep.tile([P, 1], F32, name="row_sum%d" % rt))
 
-        def sum_rows_on_vector(rt):
-            nc.vector.tensor_reduce(out=row_sums[rt][:], in_=x_tiles[rt][:], axis=AXIS.X, op=ALU.add)
-
-        for rt in range(ROW_TILES):
-            x_words = x_tiles[rt][:].bitcast(F32)
-            rows = slice(rt * P, (rt + 1) * P)
-            for first in range(0, PASSES, 2):
-                bank = turn_psum.tile([P, 2, 2, P], F32, tag="turn")
-                for gi in range(2):
-                    start_word = (first + gi) * words_a_pass
+        def turn_in(g):
+            for h in range(HALVES):
+                x_words = x_tiles[(g, h)][:].bitcast(F32)
+                bank = turn_psum.tile([P, HALF_TILES, 2, P], F32, tag="turn")
+                for i in range(HALF_TILES):
                     for u in range(2):
-                        nc.tensor.transpose(
-                            bank[:, gi, u, :],
-                            x_words[:, start_word + u : start_word + words_a_pass : 2],
-                            ident[:],
-                        )
+                        nc.tensor.transpose(bank[:, i, u, :], x_words[:, i, u:words_a_pass:2], ident[:])
+                rows = slice(h * HALF_ROWS, (h + 1) * HALF_ROWS)
                 nc.scalar.copy(
-                    out=grouped_words[:, first : first + 2, rows, :],
-                    in_=bank[:].rearrange("p g u r -> p g r u"),
-                )
-            if rt == 0:
-                sum_rows_on_vector(rt)
-            for g in range(PASSES):
-                nc.vector.quantize_mx(
-                    out=vi_codes[:, g, rows].bitcast(FP8X4),
-                    scales=vi_planes[:, g, rows],
-                    in_=grouped[:, g, rows, :].rearrange("p r t -> p (r t)"),
+                    out=grouped_words[:, g, rows, :].rearrange("p (i r) u -> p i r u", i=HALF_TILES),
+                    in_=bank[:].rearrange("p i u r -> p i r u"),
                 )
 
-        b_bank = turn_psum.tile([P, P], BF16, tag="turn")
-        nc.tensor.transpose(b_bank[:], b_rows[:], ident_bf16[:])
-        bias = keep.tile([P, OUT_TILES], F32)
-        nc.scalar.copy(out=bias[:], in_=b_bank[:, 0:OUT_TILES])
+        def quantise(g, h):
+            rows = slice(h * HALF_ROWS, (h + 1) * HALF_ROWS)
+            nc.vector.quantize_mx(
+                out=vi_codes[:, g, rows].bitcast(FP8X4),
+                scales=vi_planes[:, g, rows],
+                in_=grouped[:, g, rows, :].rearrange("p r t -> p (r t)"),
+            )
 
-        for rt in range(1, ROW_TILES - 1):
-            sum_rows_on_vector(rt)
-        unused = keep.tile([P, K], BF16)
-        nc.scalar.activation(
-            out=unused[:],
-            in_=x_tiles[ROW_TILES - 1][:],
-            func=FUNC.Copy,
-            accum_out=row_sums[ROW_TILES - 1][:],
-        )
+        row_parts = keep.tile([P, ROW_TILES, PASSES // 2], F32)
+        row_sums = keep.tile([P, ROW_TILES], F32)
+        unused = keep.tile([P, K_PASS], F32)
+
+        def sum_rows(pair, rt):
+            h, i = divmod(rt, HALF_TILES)
+            nc.vector.scalar_tensor_tensor(
+                out=unused[:],
+                in0=x_tiles[(2 * pair, h)][:, i, :],
+                scalar=1.0,
+                in1=x_tiles[(2 * pair + 1, h)][:, i, :],
+                op0=ALU.mult,
+                op1=ALU.add,
+                accum_out=row_parts[:, rt, pair : pair + 1],
+            )
+
         row_factor = keep.tile([P, ROWS], F32)
 
         def spread_row_sums():
             bank = turn_psum.tile([P, ROW_TILES, P], F32, tag="turn")
             for rt in range(ROW_TILES):
-                nc.tensor.transpose(bank[:, rt, :], row_sums[rt][:].to_broadcast([P, P]), ident[:])
+                nc.tensor.transpose(bank[:, rt, :], row_sums[:, rt : rt + 1].to_broadcast([P, P]), ident[:])
             nc.vector.tensor_scalar(
                 out=row_factor[:],
                 in0=bank[:].rearrange("p t r -> p (t r)"),
@@ -143,30 +155,40 @@ def tile_optimalnet_pb_kernel(tc, vi, W_words, W_scales, b, out_0, out_1):
                 op0=ALU.mult,
             )
 
+        acc_tiles = {}
         vj_tiles = {}
+        bias = keep.tile([P, OUT_TILES], F32)
 
-        def multiply(j):
+        def one_pass(j, g):
             rnd, i = divmod(j, RUN)
-            acc = sums_psum.tile([P, ROWS], F32, tag="acc")
-            for g in range(PASSES):
-                nc.tensor.matmul_mx(
-                    out=acc[:],
-                    lhsT=w_words[rnd][:, g, i * P * 2 : (i + 1) * P * 2].bitcast(FP4X4),
-                    lhsT_scale=w_planes[rnd][:, g, i * P : (i + 1) * P],
-                    rhs=vi_codes[:, g, :].bitcast(FP8X4),
-                    rhs_scale=vi_planes[:, g, :],
-                    start=(g == 0),
-                    stop=(g == PASSES - 1),
-                )
+            if g == 0:
+                acc = sums_psum.tile([P, ROWS], F32, tag="acc")
+                acc_tiles[j] = acc
+            nc.tensor.matmul_mx(
+                out=acc_tiles[j][:],
+                lhsT=w_words[rnd][:, g, i * P * 2 : (i + 1) * P * 2].bitcast(FP4X4),
+                lhsT_scale=w_planes[rnd][:, g, i * P : (i + 1) * P],
+                rhs=vi_codes[:, g, :].bitcast(FP8X4),
+                rhs_scale=vi_planes[:, g, :],
+                start=(g == 0),
+                stop=(g == PASSES - 1),
+            )
+
+        def relu(j):
             vj = layer.tile([P, ROWS], F32, tag="vj")
             nc.scalar.activation(
                 out=vj[:],
-                in_=acc[:],
+                in_=acc_tiles[j][:],
                 func=FUNC.Relu,
                 bias=bias[:, j : j + 1],
                 accum_out=col_sums[:, j : j + 1],
             )
             vj_tiles[j] = vj
+
+        def multiply(j):
+            for g in range(PASSES):
+                one_pass(j, g)
+            relu(j)
 
         def correct(j):
             vj = vj_tiles[j]
@@ -181,39 +203,72 @@ def tile_optimalnet_pb_kernel(tc, vi, W_words, W_scales, b, out_0, out_1):
 
         out_view = out_0.rearrange("(t r) o -> r t o", r=P)
 
-        def turn_back(rnd):
-            for first in range(rnd * RUN, (rnd + 1) * RUN, STORE_TILES):
-                result = leaving.tile([P, ROW_TILES, STORE_TILES * P], F32, tag="result")
-                for i in range(STORE_TILES):
-                    vj = vj_tiles[first + i]
-                    bank = turn_psum.tile([P, ROW_TILES, P], F32, tag="turn")
-                    for rt in range(ROW_TILES):
-                        nc.tensor.transpose(bank[:, rt, :], vj[:, rt * P : (rt + 1) * P], ident[:])
-                    if i % 2 == 0:
-                        nc.scalar.copy(out=result[:, :, i * P : (i + 1) * P], in_=bank[:])
-                    else:
-                        nc.vector.tensor_copy(out=result[:, :, i * P : (i + 1) * P], in_=bank[:])
-                nc.sync.dma_start(
-                    out=out_view[:, :, first * P : (first + STORE_TILES) * P], in_=result[:]
-                )
+        def turn_back(first):
+            result = leaving.tile([P, ROW_TILES, STORE_TILES * P], F32, tag="result")
+            for i in range(STORE_TILES):
+                vj = vj_tiles[first + i]
+                bank = turn_psum.tile([P, ROW_TILES, P], F32, tag="turn")
+                for rt in range(ROW_TILES):
+                    nc.tensor.transpose(bank[:, rt, :], vj[:, rt * P : (rt + 1) * P], ident[:])
+                if i % 2 == 0:
+                    nc.scalar.copy(out=result[:, :, i * P : (i + 1) * P], in_=bank[:])
+                else:
+                    nc.vector.tensor_copy(out=result[:, :, i * P : (i + 1) * P], in_=bank[:])
+            nc.sync.dma_start(out=out_view[:, :, first * P : (first + STORE_TILES) * P], in_=result[:])
 
-        for rnd in range(ROUNDS + 1):
-            for i in range(RUN):
-                if rnd < ROUNDS:
-                    multiply(rnd * RUN + i)
-                    if rnd > 0:
-                        correct(rnd * RUN + i)
-                if rnd > 0 and i == LAG - 1:
-                    turn_back(rnd - 1)
-            if rnd == 0:
-                spread_row_sums()
-                for j in range(RUN):
-                    correct(j)
+        def store_means():
+            mean_bank = turn_psum.tile([P, P], F32, tag="turn")
+            nc.tensor.transpose(mean_bank[:], col_sums[:], ident[:])
+            means = keep.tile([P, P], F32)
+            nc.scalar.activation(
+                out=means[0:OUT_TILES, :], in_=mean_bank[0:OUT_TILES, :], func=FUNC.Copy, scale=1.0 / ROWS
+            )
+            nc.sync.dma_start(out=out_1.rearrange("(j p) -> j p", p=P), in_=means[0:OUT_TILES, :])
 
-        mean_bank = turn_psum.tile([P, P], F32, tag="turn")
-        nc.tensor.transpose(mean_bank[:], col_sums[:], ident[:])
-        means = keep.tile([P, P], F32)
-        nc.scalar.activation(
-            out=means[0:OUT_TILES, :], in_=mean_bank[0:OUT_TILES, :], func=FUNC.Copy, scale=1.0 / ROWS
-        )
-        nc.sync.dma_start(out=out_1.rearrange("(j p) -> j p", p=P), in_=means[0:OUT_TILES, :])
+        turn_in(0)
+        quantise(0, 0)
+        quantise(0, 1)
+        turn_in(1)
+        b_bank = turn_psum.tile([P, P], BF16, tag="turn")
+        nc.tensor.transpose(b_bank[:], b_rows[:], ident_bf16[:])
+        nc.scalar.copy(out=bias[:], in_=b_bank[:, 0:OUT_TILES])
+        quantise(1, 0)
+        quantise(1, 1)
+        sum_rows(0, 0)
+        sum_rows(0, 1)
+        for j in range(RUN):
+            one_pass(j, 0)
+        turn_in(2)
+        quantise(2, 0)
+        sum_rows(0, 2)
+        quantise(2, 1)
+        for j in range(RUN):
+            one_pass(j, 1)
+        turn_in(3)
+        sum_rows(0, 3)
+        quantise(3, 0)
+        quantise(3, 1)
+        for j in range(RUN):
+            one_pass(j, 2)
+        for j in range(RUN):
+            one_pass(j, 3)
+            relu(j)
+        for rt in range(ROW_TILES):
+            sum_rows(1, rt)
+        nc.vector.tensor_reduce(out=row_sums[:], in_=row_parts[:], axis=AXIS.X, op=ALU.add)
+
+        multiply(4)
+        multiply(5)
+        spread_row_sums()
+        for j in range(6):
+            correct(j)
+        turned = 0
+        for j in range(6, OUT_TILES):
+            multiply(j)
+            correct(j)
+            if j == min(7 + 3 * (turned // RUN), OUT_TILES - 1):
+                turn_back(turned)
+                if j == OUT_TILES - 1:
+                    store_means()
+                turn_back(turned + STORE_TILES)
+                turned += RUN

@@ -49,6 +49,8 @@ def tile_optimalnet_pb_kernel(tc, vi, W_words, W_scales, b, out_0, out_1):
         make_identity(nc, ident[:])
         ident_bf16 = keep.tile([P, P], BF16)
         make_identity(nc, ident_bf16[:])
+        zeros = keep.tile([P, ROWS], BF16)
+        nc.vector.memset(zeros[:], 0.0)
         w_planes = []
         for rnd in range(ROUNDS):
             planes = keep.tile([P, PASSES, RUN * P], U8, name="w_planes%d" % rnd, align_bytes=64)
@@ -225,9 +227,16 @@ def tile_optimalnet_pb_kernel(tc, vi, W_words, W_scales, b, out_0, out_1):
             )
             nc.sync.dma_start(out=out_1.rearrange("(j p) -> j p", p=P), in_=means[0:OUT_TILES, :])
 
+        def keep_busy(count):
+            idle_bank = sums_psum.tile([P, ROWS], F32, tag="acc")
+            for repeat in range(count):
+                nc.tensor.matmul(out=idle_bank[:], lhsT=zeros[:, 0:P], rhs=zeros[:], start=True, stop=True)
+
+        keep_busy(5)
         turn_in(0)
         quantise(0, 0)
         quantise(0, 1)
+        keep_busy(2)
         turn_in(1)
         b_bank = turn_psum.tile([P, P], BF16, tag="turn")
         nc.tensor.transpose(b_bank[:], b_rows[:], ident_bf16[:])

@@ -45,12 +45,12 @@ def tile_optimalnet_pb_kernel(tc, vi, W_words, W_scales, b, out_0, out_1):
         sums_psum = stack.enter_context(tc.psum_pool(name="sums_psum", bufs=4))
         turn_psum = stack.enter_context(tc.psum_pool(name="turn_psum", bufs=4))
 
+        zeros = keep.tile([P, ROWS], BF16)
+        nc.gpsimd.memset(zeros[:], 0.0)
         ident = keep.tile([P, P], F32)
         make_identity(nc, ident[:])
         ident_bf16 = keep.tile([P, P], BF16)
         make_identity(nc, ident_bf16[:])
-        zeros = keep.tile([P, ROWS], BF16)
-        nc.vector.memset(zeros[:], 0.0)
         w_planes = []
         for rnd in range(ROUNDS):
             planes = keep.tile([P, PASSES, RUN * P], U8, name="w_planes%d" % rnd, align_bytes=64)
@@ -192,31 +192,56 @@ def tile_optimalnet_pb_kernel(tc, vi, W_words, W_scales, b, out_0, out_1):
                 one_pass(j, g)
             relu(j)
 
-        def correct(j):
+        def correct(j, pieces=1):
             vj = vj_tiles[j]
-            nc.vector.scalar_tensor_tensor(
-                out=vj[:],
-                in0=row_factor[:],
-                scalar=col_sums[:, j : j + 1],
-                in1=vj[:],
-                op0=ALU.mult,
-                op1=ALU.add,
-            )
+            width = ROWS // pieces
+            for piece in range(pieces):
+                cols = slice(piece * width, (piece + 1) * width)
+                nc.vector.scalar_tensor_tensor(
+                    out=vj[:, cols],
+                    in0=row_factor[:, cols],
+                    scalar=col_sums[:, j : j + 1],
+                    in1=vj[:, cols],
+                    op0=ALU.mult,
+                    op1=ALU.add,
+                )
 
         out_view = out_0.rearrange("(t r) o -> r t o", r=P)
 
-        def turn_back(first):
+        def turn_back(first, scalar_only=False):
             result = leaving.tile([P, ROW_TILES, STORE_TILES * P], F32, tag="result")
             for i in range(STORE_TILES):
                 vj = vj_tiles[first + i]
                 bank = turn_psum.tile([P, ROW_TILES, P], F32, tag="turn")
                 for rt in range(ROW_TILES):
                     nc.tensor.transpose(bank[:, rt, :], vj[:, rt * P : (rt + 1) * P], ident[:])
-                if i % 2 == 0:
+                if i % 2 == 0 or scalar_only:
                     nc.scalar.copy(out=result[:, :, i * P : (i + 1) * P], in_=bank[:])
                 else:
                     nc.vector.tensor_copy(out=result[:, :, i * P : (i + 1) * P], in_=bank[:])
             nc.sync.dma_start(out=out_view[:, :, first * P : (first + STORE_TILES) * P], in_=result[:])
+
+        def turn_back_last(first):
+            banks = []
+            for h in range(HALVES):
+                bank = turn_psum.tile([P, HALF_TILES, STORE_TILES, P], F32, tag="turn")
+                banks.append(bank)
+            for i in range(STORE_TILES):
+                vj = vj_tiles[first + i]
+                for rt in range(ROW_TILES):
+                    nc.tensor.transpose(
+                        banks[rt // HALF_TILES][:, rt % HALF_TILES, i, :], vj[:, rt * P : (rt + 1) * P], ident[:]
+                    )
+            for h in range(HALVES):
+                result = leaving.tile([P, HALF_TILES, STORE_TILES * P], F32, tag="result")
+                if h == 0:
+                    nc.vector.tensor_copy(out=result[:], in_=banks[h][:].rearrange("p t i o -> p t (i o)"))
+                else:
+                    nc.scalar.copy(out=result[:], in_=banks[h][:].rearrange("p t i o -> p t (i o)"))
+                nc.sync.dma_start(
+                    out=out_view[:, h * HALF_TILES : (h + 1) * HALF_TILES, first * P : (first + STORE_TILES) * P],
+                    in_=result[:],
+                )
 
         def store_means():
             mean_bank = turn_psum.tile([P, P], F32, tag="turn")
@@ -232,7 +257,7 @@ def tile_optimalnet_pb_kernel(tc, vi, W_words, W_scales, b, out_0, out_1):
             for repeat in range(count):
                 nc.tensor.matmul(out=idle_bank[:], lhsT=zeros[:, 0:P], rhs=zeros[:], start=True, stop=True)
 
-        keep_busy(5)
+        keep_busy(6)
         turn_in(0)
         quantise(0, 0)
         quantise(0, 1)
@@ -272,12 +297,15 @@ def tile_optimalnet_pb_kernel(tc, vi, W_words, W_scales, b, out_0, out_1):
         for j in range(6):
             correct(j)
         turned = 0
-        for j in range(6, OUT_TILES):
+        for j in range(6, OUT_TILES - 1):
             multiply(j)
             correct(j)
-            if j == min(7 + 3 * (turned // RUN), OUT_TILES - 1):
+            if j == 7 + 3 * (turned // RUN):
                 turn_back(turned)
-                if j == OUT_TILES - 1:
-                    store_means()
                 turn_back(turned + STORE_TILES)
                 turned += RUN
+        multiply(OUT_TILES - 1)
+        correct(OUT_TILES - 1, pieces=2)
+        turn_back(turned, scalar_only=True)
+        store_means()
+        turn_back_last(turned + STORE_TILES)

@@ -32,6 +32,9 @@ HALF_TILES = 2
 HALVES = ROW_TILES // HALF_TILES
 HALF_ROWS = HALF_TILES * P
 
+BLOCK = 32
+BY_VECTOR = (4, 5, 10, 11)
+
 FLOPS = 2 * ROWS * K * OUTS
 
 
@@ -177,7 +180,7 @@ def tile_optimalnet_pb_kernel(tc, vi, W_words, W_scales, b, out_0, out_1):
             )
 
         def relu(j):
-            vj = layer.tile([P, ROWS], F32, tag="vj")
+            vj = layer.tile([P, ROWS], F32, tag="vj", align_bytes=64)
             nc.scalar.activation(
                 out=vj[:],
                 in_=acc_tiles[j][:],
@@ -243,6 +246,17 @@ def tile_optimalnet_pb_kernel(tc, vi, W_words, W_scales, b, out_0, out_1):
                     in_=result[:],
                 )
 
+        out_blocks = out_0.rearrange("(rb a) (j ob b) -> j ob a rb b", a=BLOCK, ob=P // BLOCK, b=BLOCK)
+
+        def leave_by_vector(j):
+            turned_blocks = leaving.tile([P, ROWS], F32, tag="blocks", align_bytes=64)
+            nc.vector.transpose(out=turned_blocks[:], in_=vj_tiles[j][:])
+            for ob in range(P // BLOCK):
+                nc.sync.dma_start(
+                    out=out_blocks[j][ob],
+                    in_=turned_blocks[ob * BLOCK : (ob + 1) * BLOCK, :].rearrange("a (rb b) -> a rb b", b=BLOCK),
+                )
+
         def store_means():
             mean_bank = turn_psum.tile([P, P], F32, tag="turn")
             nc.tensor.transpose(mean_bank[:], col_sums[:], ident[:])
@@ -296,14 +310,20 @@ def tile_optimalnet_pb_kernel(tc, vi, W_words, W_scales, b, out_0, out_1):
         spread_row_sums()
         for j in range(6):
             correct(j)
-        turned = 0
+        leave_by_vector(4)
+        leave_by_vector(5)
         for j in range(6, OUT_TILES - 1):
             multiply(j)
             correct(j)
-            if j == 7 + 3 * (turned // RUN):
-                turn_back(turned)
-                turn_back(turned + STORE_TILES)
-                turned += RUN
+            if j in BY_VECTOR:
+                leave_by_vector(j)
+            if j == 7:
+                turn_back(0)
+                turn_back(2)
+            if j == 11:
+                turn_back(6)
+                turn_back(8)
+        turned = 12
         multiply(OUT_TILES - 1)
         correct(OUT_TILES - 1, pieces=2)
         turn_back(turned, scalar_only=True)

@@ -280,6 +280,7 @@ def tile_optimalnet_pb_kernel(tc, vi, W_words, W_scales, b, out_0, out_1):
         b_bank = turn_psum.tile([P, P], BF16, tag="turn")
         nc.tensor.transpose(b_bank[:], b_rows[:], ident_bf16[:])
         nc.scalar.copy(out=bias[:], in_=b_bank[:, 0:OUT_TILES])
+        keep_busy(2)
         quantise(1, 0)
         quantise(1, 1)
         sum_rows(0, 0)

@@ -112,18 +112,33 @@ def tile_optimalnet_pb_kernel(tc, vi, W_words, W_scales, b, out_0, out_1):
         def turn_in(g):
             for h in range(HALVES):
                 x_words = x_tiles[(g, h)][:].bitcast(F32)
-                bank = turn_psum.tile([P, HALF_TILES, 2, P], F32, tag="turn")
-                for i in range(HALF_TILES):
-                    for u in range(2):
-                        nc.tensor.transpose(bank[:, i, u, :], x_words[:, i, u:words_a_pass:2], ident[:])
-                rows = slice(h * HALF_ROWS, (h + 1) * HALF_ROWS)
-                nc.scalar.copy(
-                    out=grouped_words[:, g, rows, :].rearrange("p (i r) u -> p i r u", i=HALF_TILES),
-                    in_=bank[:].rearrange("p i u r -> p i r u"),
-                )
+                if g == PASSES - 1 and h == HALVES - 1:
+                    for i in range(HALF_TILES):
+                        small_bank = turn_psum.tile([P, 2, P], F32, tag="turn")
+                        for u in range(2):
+                            nc.tensor.transpose(small_bank[:, u, :], x_words[:, i, u:words_a_pass:2], ident[:])
+                        rt = h * HALF_TILES + i
+                        nc.scalar.copy(
+                            out=grouped_words[:, g, rt * P : (rt + 1) * P, :],
+                            in_=small_bank[:].rearrange("p u r -> p r u"),
+                        )
+                else:
+                    bank = turn_psum.tile([P, HALF_TILES, 2, P], F32, tag="turn")
+                    for i in range(HALF_TILES):
+                        for u in range(2):
+                            nc.tensor.transpose(bank[:, i, u, :], x_words[:, i, u:words_a_pass:2], ident[:])
+                    rows = slice(h * HALF_ROWS, (h + 1) * HALF_ROWS)
+                    nc.scalar.copy(
+                        out=grouped_words[:, g, rows, :].rearrange("p (i r) u -> p i r u", i=HALF_TILES),
+                        in_=bank[:].rearrange("p i u r -> p i r u"),
+                    )
 
-        def quantise(g, h):
-            rows = slice(h * HALF_ROWS, (h + 1) * HALF_ROWS)
+        def quantise(g, h, pieces=1):
+            for piece in range(pieces):
+                quantise_rows(g, h * HALF_ROWS + piece * (HALF_ROWS // pieces), HALF_ROWS // pieces)
+
+        def quantise_rows(g, first_row, count):
+            rows = slice(first_row, first_row + count)
             nc.vector.quantize_mx(
                 out=vi_codes[:, g, rows].bitcast(FP8X4),
                 scales=vi_planes[:, g, rows],
@@ -296,7 +311,7 @@ def tile_optimalnet_pb_kernel(tc, vi, W_words, W_scales, b, out_0, out_1):
         turn_in(3)
         sum_rows(0, 3)
         quantise(3, 0)
-        quantise(3, 1)
+        quantise(3, 1, pieces=HALF_TILES)
         for j in range(RUN):
             one_pass(j, 2)
         for j in range(RUN):

from contextlib import ExitStack

import concourse.mybir as mybir
from concourse.masks import make_identity

F32 = mybir.dt.float32
BF16 = mybir.dt.bfloat16
I32 = mybir.dt.int32
U32 = mybir.dt.uint32
U8 = mybir.dt.uint8
FP8X4 = mybir.dt.float8_e4m3fn_x4
FP4X4 = mybir.dt.float4_e2m1fn_x4
FUNC = mybir.ActivationFunctionType
ALU = mybir.AluOpType
AXIS = mybir.AxisListType

P = 128
PACK = 4
K_PASS = P * PACK
ROWS = 512
K = 2048
OUTS = 2048
ROW_TILES = ROWS // P
PASSES = K // K_PASS
OUT_TILES = OUTS // P
C = 0.01 * 0.001 / 1

RUN = 4
ROUNDS = OUT_TILES // RUN
STORE_TILES = 2
HALF_TILES = 2
HALVES = ROW_TILES // HALF_TILES
HALF_ROWS = HALF_TILES * P

BLOCK = 32
BY_VECTOR = (4, 5, 10, 11)

FLOPS = 2 * ROWS * K * OUTS


def tile_optimalnet_pb_kernel(tc, vi, W_words, W_scales, b, out_0, out_1):
    nc = tc.nc
    with ExitStack() as stack:
        stack.enter_context(tc.manual_schedule())
        keep = stack.enter_context(tc.tile_pool(name="keep", bufs=1))
        layer = stack.enter_context(tc.tile_pool(name="layer", bufs=10))
        leaving = stack.enter_context(tc.tile_pool(name="leaving", bufs=4))
        sums_psum = stack.enter_context(tc.psum_pool(name="sums_psum", bufs=4))
        turn_psum = stack.enter_context(tc.psum_pool(name="turn_psum", bufs=4))

        zeros = keep.tile([P, ROWS], BF16)
        nc.gpsimd.memset(zeros[:], 0.0)
        ident = keep.tile([P, P], F32)
        make_identity(nc, ident[:])
        ident_bf16 = keep.tile([P, P], BF16)
        make_identity(nc, ident_bf16[:])
        w_planes = []
        for rnd in range(ROUNDS):
            planes = keep.tile([P, PASSES, RUN * P], U8, name="w_planes%d" % rnd, align_bytes=64)
            w_planes.append(planes)
        nc.vector.memset(w_planes[0][:].bitcast(I32), 0)
        b_rows = keep.tile([P, P], BF16)
        nc.vector.memset(b_rows[:], 0.0)
        col_sums = keep.tile([P, P], F32)
        nc.vector.memset(col_sums[:], 0.0)
        for rnd in range(1, ROUNDS):
            nc.vector.memset(w_planes[rnd][:].bitcast(I32), 0)

        nc.scalar.dma_start(out=b_rows[0:OUT_TILES, :], in_=b.rearrange("(j p) -> j p", p=P))
        x_view = vi.rearrange("(h i r) k -> h r i k", i=HALF_TILES, r=P)
        x_tiles = {}

        def load_x(g):
            for h in range(HALVES):
                x = keep.tile([P, HALF_TILES, K_PASS], BF16, name="x%d_%d" % (g, h))
                nc.sync.dma_start(out=x[:], in_=x_view[h][:, :, g * K_PASS : (g + 1) * K_PASS])
                x_tiles[(g, h)] = x

        words_dram = W_words.bitcast(I32).rearrange("g p n -> p g n")
        scales_dram = W_scales.bitcast(I32).rearrange("g (q r) n -> r q g n", r=4)
        w_words = {}

        def load_scales(rnd):
            plane_cols = slice(rnd * RUN * P // 4, (rnd + 1) * RUN * P // 4)
            for r in range(4):
                nc.sync.dma_start(
                    out=w_planes[rnd][:].bitcast(I32)[r:P:32], in_=scales_dram[r][:, :, plane_cols]
                )

        def load_words(rnd):
            words = keep.tile([P, PASSES, RUN * P * 2], U8, name="w_words%d" % rnd, align_bytes=64)
            word_cols = slice(rnd * RUN * P // 2, (rnd + 1) * RUN * P // 2)
            nc.sync.dma_start(out=words[:].bitcast(I32), in_=words_dram[:, :, word_cols])
            w_words[rnd] = words

        load_x(0)
        load_scales(0)
        load_x(1)
        load_words(0)
        load_x(2)
        load_x(3)
        for rnd in range(1, ROUNDS):
            load_scales(rnd)
            load_words(rnd)

        grouped = keep.tile([P, PASSES, ROWS, PACK], BF16, align_bytes=64)
        grouped_words = grouped[:].bitcast(F32)
        vi_codes = keep.tile([P, PASSES, ROWS], U32, align_bytes=64)
        vi_planes = keep.tile([P, PASSES, ROWS], U8, align_bytes=64)
        words_a_pass = K_PASS // 2

        def turn_in(g):
            for h in range(HALVES):
                x_words = x_tiles[(g, h)][:].bitcast(F32)
                if g == PASSES - 1 and h == HALVES - 1:
                    for i in range(HALF_TILES):
                        small_bank = turn_psum.tile([P, 2, P], F32, tag="turn")
                        for u in range(2):
                            nc.tensor.transpose(small_bank[:, u, :], x_words[:, i, u:words_a_pass:2], ident[:])
                        rt = h * HALF_TILES + i
                        nc.scalar.copy(
                            out=grouped_words[:, g, rt * P : (rt + 1) * P, :],
                            in_=small_bank[:].rearrange("p u r -> p r u"),
                        )
                else:
                    bank = turn_psum.tile([P, HALF_TILES, 2, P], F32, tag="turn")
                    for i in range(HALF_TILES):
                        for u in range(2):
                            nc.tensor.transpose(bank[:, i, u, :], x_words[:, i, u:words_a_pass:2], ident[:])
                    rows = slice(h * HALF_ROWS, (h + 1) * HALF_ROWS)
                    nc.scalar.copy(
                        out=grouped_words[:, g, rows, :].rearrange("p (i r) u -> p i r u", i=HALF_TILES),
                        in_=bank[:].rearrange("p i u r -> p i r u"),
                    )

        def quantise(g, h, pieces=1):
            for piece in range(pieces):
                quantise_rows(g, h * HALF_ROWS + piece * (HALF_ROWS // pieces), HALF_ROWS // pieces)

        def quantise_rows(g, first_row, count):
            rows = slice(first_row, first_row + count)
            nc.vector.quantize_mx(
                out=vi_codes[:, g, rows].bitcast(FP8X4),
                scales=vi_planes[:, g, rows],
                in_=grouped[:, g, rows, :].rearrange("p r t -> p (r t)"),
            )

        row_parts = keep.tile([P, ROW_TILES, PASSES // 2], F32)
        row_sums = keep.tile([P, ROW_TILES], F32)
        unused = keep.tile([P, K_PASS], F32)

        def sum_rows(pair, rt):
            h, i = divmod(rt, HALF_TILES)
            nc.vector.scalar_tensor_tensor(
                out=unused[:],
                in0=x_tiles[(2 * pair, h)][:, i, :],
                scalar=1.0,
                in1=x_tiles[(2 * pair + 1, h)][:, i, :],
                op0=ALU.mult,
                op1=ALU.add,
                accum_out=row_parts[:, rt, pair : pair + 1],
            )

        row_factor = keep.tile([P, ROWS], F32)

        def spread_row_sums():
            bank = turn_psum.tile([P, ROW_TILES, P], F32, tag="turn")
            for rt in range(ROW_TILES):
                nc.tensor.transpose(bank[:, rt, :], row_sums[:, rt : rt + 1].to_broadcast([P, P]), ident[:])
            nc.vector.tensor_scalar(
                out=row_factor[:],
                in0=bank[:].rearrange("p t r -> p (t r)"),
                scalar1=C / ROWS,
                scalar2=None,
                op0=ALU.mult,
            )

        acc_tiles = {}
        vj_tiles = {}
        bias = keep.tile([P, OUT_TILES], F32)

        def one_pass(j, g):
            rnd, i = divmod(j, RUN)
            if g == 0:
                acc = sums_psum.tile([P, ROWS], F32, tag="acc")
                acc_tiles[j] = acc
            nc.tensor.matmul_mx(
                out=acc_tiles[j][:],
                lhsT=w_words[rnd][:, g, i * P * 2 : (i + 1) * P * 2].bitcast(FP4X4),
                lhsT_scale=w_planes[rnd][:, g, i * P : (i + 1) * P],
                rhs=vi_codes[:, g, :].bitcast(FP8X4),
                rhs_scale=vi_planes[:, g, :],
                start=(g == 0),
                stop=(g == PASSES - 1),
            )

        def relu(j):
            vj = layer.tile([P, ROWS], F32, tag="vj", align_bytes=64)
            nc.scalar.activation(
                out=vj[:],
                in_=acc_tiles[j][:],
                func=FUNC.Relu,
                bias=bias[:, j : j + 1],
                accum_out=col_sums[:, j : j + 1],
            )
            vj_tiles[j] = vj

        def multiply(j):
            for g in range(PASSES):
                one_pass(j, g)
            relu(j)

        def correct(j, pieces=1):
            vj = vj_tiles[j]
            width = ROWS // pieces
            for piece in range(pieces):
                cols = slice(piece * width, (piece + 1) * width)
                nc.vector.scalar_tensor_tensor(
                    out=vj[:, cols],
                    in0=row_factor[:, cols],
                    scalar=col_sums[:, j : j + 1],
                    in1=vj[:, cols],
                    op0=ALU.mult,
                    op1=ALU.add,
                )

        out_view = out_0.rearrange("(t r) o -> r t o", r=P)

        def turn_back(first, scalar_only=False):
            result = leaving.tile([P, ROW_TILES, STORE_TILES * P], F32, tag="result")
            for i in range(STORE_TILES):
                vj = vj_tiles[first + i]
                bank = turn_psum.tile([P, ROW_TILES, P], F32, tag="turn")
                for rt in range(ROW_TILES):
                    nc.tensor.transpose(bank[:, rt, :], vj[:, rt * P : (rt + 1) * P], ident[:])
                if i % 2 == 0 or scalar_only:
                    nc.scalar.copy(out=result[:, :, i * P : (i + 1) * P], in_=bank[:])
                else:
                    nc.vector.tensor_copy(out=result[:, :, i * P : (i + 1) * P], in_=bank[:])
            nc.sync.dma_start(out=out_view[:, :, first * P : (first + STORE_TILES) * P], in_=result[:])

        def turn_back_last(first):
            banks = []
            for h in range(HALVES):
                bank = turn_psum.tile([P, HALF_TILES, STORE_TILES, P], F32, tag="turn")
                banks.append(bank)
            for i in range(STORE_TILES):
                vj = vj_tiles[first + i]
                for rt in range(ROW_TILES):
                    nc.tensor.transpose(
                        banks[rt // HALF_TILES][:, rt % HALF_TILES, i, :], vj[:, rt * P : (rt + 1) * P], ident[:]
                    )
            for h in range(HALVES):
                result = leaving.tile([P, HALF_TILES, STORE_TILES * P], F32, tag="result")
                if h == 0:
                    nc.vector.tensor_copy(out=result[:], in_=banks[h][:].rearrange("p t i o -> p t (i o)"))
                else:
                    nc.scalar.copy(out=result[:], in_=banks[h][:].rearrange("p t i o -> p t (i o)"))
                nc.sync.dma_start(
                    out=out_view[:, h * HALF_TILES : (h + 1) * HALF_TILES, first * P : (first + STORE_TILES) * P],
                    in_=result[:],
                )

        out_blocks = out_0.rearrange("(rb a) (j ob b) -> j ob a rb b", a=BLOCK, ob=P // BLOCK, b=BLOCK)

        def leave_by_vector(j):
            turned_blocks = leaving.tile([P, ROWS], F32, tag="blocks", align_bytes=64)
            nc.vector.transpose(out=turned_blocks[:], in_=vj_tiles[j][:])
            for ob in range(P // BLOCK):
                nc.sync.dma_start(
                    out=out_blocks[j][ob],
                    in_=turned_blocks[ob * BLOCK : (ob + 1) * BLOCK, :].rearrange("a (rb b) -> a rb b", b=BLOCK),
                )

        def store_means():
            mean_bank = turn_psum.tile([P, P], F32, tag="turn")
            nc.tensor.transpose(mean_bank[:], col_sums[:], ident[:])
            means = keep.tile([P, P], F32)
            nc.scalar.activation(
                out=means[0:OUT_TILES, :], in_=mean_bank[0:OUT_TILES, :], func=FUNC.Copy, scale=1.0 / ROWS
            )
            nc.sync.dma_start(out=out_1.rearrange("(j p) -> j p", p=P), in_=means[0:OUT_TILES, :])

        def keep_busy(count):
            idle_bank = sums_psum.tile([P, ROWS], F32, tag="acc")
            for repeat in range(count):
                nc.tensor.matmul(out=idle_bank[:], lhsT=zeros[:, 0:P], rhs=zeros[:], start=True, stop=True)

        keep_busy(6)
        turn_in(0)
        quantise(0, 0)
        quantise(0, 1)
        keep_busy(2)
        turn_in(1)
        b_bank = turn_psum.tile([P, P], BF16, tag="turn")
        nc.tensor.transpose(b_bank[:], b_rows[:], ident_bf16[:])
        nc.scalar.copy(out=bias[:], in_=b_bank[:, 0:OUT_TILES])
        keep_busy(2)
        quantise(1, 0)
        quantise(1, 1)
        sum_rows(0, 0)
        sum_rows(0, 1)
        for j in range(RUN):
            one_pass(j, 0)
        turn_in(2)
        quantise(2, 0)
        sum_rows(0, 2)
        quantise(2, 1)
        for j in range(RUN):
            one_pass(j, 1)
        turn_in(3)
        sum_rows(0, 3)
        quantise(3, 0)
        quantise(3, 1, pieces=HALF_TILES)
        for j in range(RUN):
            one_pass(j, 2)
        for j in range(RUN):
            one_pass(j, 3)
            relu(j)
        for rt in range(ROW_TILES):
            sum_rows(1, rt)
        nc.vector.tensor_reduce(out=row_sums[:], in_=row_parts[:], axis=AXIS.X, op=ALU.add)

        multiply(4)
        multiply(5)
        spread_row_sums()
        for j in range(6):
            correct(j)
        leave_by_vector(4)
        leave_by_vector(5)
        for j in range(6, OUT_TILES - 1):
            multiply(j)
            correct(j)
            if j in BY_VECTOR:
                leave_by_vector(j)
            if j == 7:
                turn_back(0)
                turn_back(2)
            if j == 11:
                turn_back(6)
                turn_back(8)
        turned = 12
        multiply(OUT_TILES - 1)
        correct(OUT_TILES - 1, pieces=2)
        turn_back(turned, scalar_only=True)
        store_means()
        turn_back_last(turned + STORE_TILES)
